import numpy as np
import ml_dtypes

BF16 = ml_dtypes.bfloat16


def bf(x):
    return np.asarray(x, np.float32).astype(BF16)


def f32(x):
    return np.asarray(x, np.float32)


def f64(x):
    return np.asarray(x).astype(np.float64)


def striped(idx):
    return np.tile(idx.reshape(-1, 16).T, (8, 1))


D, S, N, H = 768, 4096, 2048, 12
SLOPE = 0.01


def leaky(t):
    return np.maximum(t, SLOPE * t)


def unit(t):
    t3 = t.reshape(H, D // H, -1)
    return (t3 / np.sqrt((t3 * t3).sum(axis=1, keepdims=True))).reshape(D, -1)


def weight():
    return bf(np.random.standard_normal((D, D)) * np.sqrt(2.0 / D))


def bias():
    return f32(0.1 * np.random.standard_normal((D, 1)))


def setup_inputs():
    return {"emb": f32(np.random.standard_normal((D, S))), "w_q": weight(), "b_q": bias(), "w_k": weight(), "b_k": bias(), "w_v": weight(), "b_v": bias(), "offs": striped(np.random.permutation(S)[:N])}


def reference(emb, w_q, b_q, w_k, b_k, w_v, b_v, offs):
    idx = offs[:16].T.reshape(-1)
    a = leaky(f64(emb)[:, idx])
    qh = leaky(f64(w_q).T @ a + f64(b_q))
    kh = leaky(f64(w_k).T @ a + f64(b_k))
    vh = leaky(f64(w_v).T @ a + f64(b_v))
    return np.concatenate([unit(qh), unit(kh), vh], axis=0)

@@ -1,0 +1,114 @@
+import concourse.mybir as mybir
+
+F32 = mybir.dt.float32
+BF16 = mybir.dt.bfloat16
+U16 = mybir.dt.uint16
+ACT = mybir.ActivationFunctionType
+ALU = mybir.AluOpType
+
+P = 128
+D = 768
+S = 4096
+N = 2048
+HEAD = 64
+SLOPE = 0.01
+BLOCKS = D // P
+PIECE = 512
+PIECES = N // PIECE
+OFFS_COLS = PIECE // 16
+
+FLOPS = 2 * 3 * D * D * N
+
+
+def tile_etcmodel_b_kernel(tc, emb, w_q, b_q, w_k, b_k, w_v, b_v, offs, out):
+    nc = tc.nc
+    with (
+        tc.tile_pool(name="held", bufs=1) as held,
+        tc.tile_pool(name="work", bufs=4) as work,
+        tc.psum_pool(name="products", bufs=6) as products,
+        tc.psum_pool(name="lengths", bufs=2) as lengths,
+    ):
+        offsets = held.tile([P, N // 16], U16, name="offsets")
+        nc.sync.dma_start(offsets[:], offs)
+
+        table = [held.tile([P, S], F32, name=f"table{k}") for k in range(BLOCKS)]
+        weights = {}
+        for name in ("q", "k", "v"):
+            weights[name] = held.tile([P, BLOCKS, D], BF16, name=f"w_{name}")
+
+        def load_weights(name, w):
+            nc.sync.dma_start(weights[name][:], w.rearrange("(k p) m -> p k m", p=P))
+
+        nc.sync.dma_start(table[0][:], emb[0:P, :])
+        load_weights("q", w_q)
+        for k in range(1, BLOCKS):
+            nc.sync.dma_start(table[k][:], emb[k * P : (k + 1) * P, :])
+        load_weights("k", w_k)
+        load_weights("v", w_v)
+
+        bias = {}
+        low_bias = {}
+        for name, b in (("q", b_q), ("k", b_k), ("v", b_v)):
+            bias[name] = held.tile([P, BLOCKS], F32, name=f"b_{name}")
+            with nc.allow_non_contiguous_dma(reason="one bias value to a partition"):
+                nc.scalar.dma_start(bias[name][:], b.rearrange("(a p) o -> p (a o)", p=P))
+            low_bias[name] = held.tile([P, BLOCKS], F32, name=f"low_b_{name}")
+            nc.vector.tensor_scalar_mul(low_bias[name][:], bias[name][:], SLOPE)
+
+        head_ones = held.tile([P, P], BF16, name="head_ones")
+        nc.vector.memset(head_ones[:], 0.0)
+        nc.vector.memset(head_ones[0:HEAD, 0:HEAD], 1.0)
+        nc.vector.memset(head_ones[HEAD:P, HEAD:P], 1.0)
+
+        a = [[held.tile([P, PIECE], BF16, name=f"a{k}_{j}") for j in range(PIECES)] for k in range(BLOCKS)]
+        for k in range(BLOCKS):
+            for j in range(PIECES):
+                picked = work.tile([P, PIECE], F32, name="picked")
+                nc.scalar.activation(
+                    picked[:],
+                    table[k][:].indirect(offsets[:, j * OFFS_COLS : (j + 1) * OFFS_COLS]),
+                    ACT.Copy,
+                )
+                nc.vector.scalar_tensor_tensor(
+                    out=a[k][j][:], in0=picked[:], scalar=SLOPE, in1=picked[:], op0=ALU.mult, op1=ALU.max
+                )
+
+        for j in range(PIECES):
+            cols = slice(j * PIECE, (j + 1) * PIECE)
+            for part, name in enumerate(("q", "k", "v")):
+                for m in range(BLOCKS):
+                    rows = slice(part * D + m * P, part * D + (m + 1) * P)
+                    product = products.tile([P, PIECE], F32, name="product")
+                    for k in range(BLOCKS):
+                        nc.tensor.matmul(
+                            product[:],
+                            weights[name][:, k, m * P : (m + 1) * P],
+                            a[k][j][:],
+                            start=(k == 0),
+                            stop=(k == BLOCKS - 1),
+                        )
+                    low = work.tile([P, PIECE], F32, name="low")
+                    nc.scalar.activation(
+                        low[:], product[:], ACT.Identity, bias=low_bias[name][:, m : m + 1], scale=SLOPE
+                    )
+                    hidden = work.tile([P, PIECE], F32, name="hidden")
+                    nc.vector.scalar_tensor_tensor(
+                        out=hidden[:],
+                        in0=product[:],
+                        scalar=bias[name][:, m : m + 1],
+                        in1=low[:],
+                        op0=ALU.add,
+                        op1=ALU.max,
+                    )
+                    if name == "v":
+                        nc.sync.dma_start(out[rows, cols], hidden[:])
+                        continue
+                    squares = work.tile([P, PIECE], BF16, name="squares")
+                    nc.gpsimd.tensor_tensor(squares[:], hidden[:], hidden[:], ALU.mult)
+                    length2 = lengths.tile([P, PIECE], F32, name="length2")
+                    nc.tensor.matmul(length2[:], head_ones[:], squares[:], start=True, stop=True)
+                    inverse = work.tile([P, PIECE], F32, name="inverse")
+                    nc.scalar.activation(inverse[:], length2[:], ACT.Abs_reciprocal_sqrt)
+                    unit = work.tile([P, PIECE], F32, name="unit")
+                    nc.vector.tensor_tensor(unit[:], hidden[:], inverse[:], ALU.mult)
+                    nc.sync.dma_start(out[rows, cols], unit[:])

@@ -16,6 +16,7 @@ BLOCKS = D // P
 PIECE = 512
 PIECES = N // PIECE
 OFFS_COLS = PIECE // 16
+LAG = 3
 
 FLOPS = 2 * 3 * D * D * N
 
@@ -25,6 +26,7 @@ def tile_etcmodel_b_kernel(tc, emb, w_q, b_q, w_k, b_k, w_v, b_v, offs, out):
     with (
         tc.tile_pool(name="held", bufs=1) as held,
         tc.tile_pool(name="work", bufs=4) as work,
+        tc.tile_pool(name="kept", bufs=LAG + 3) as kept,
         tc.psum_pool(name="products", bufs=6) as products,
         tc.psum_pool(name="lengths", bufs=2) as lengths,
     ):
@@ -61,54 +63,64 @@ def tile_etcmodel_b_kernel(tc, emb, w_q, b_q, w_k, b_k, w_v, b_v, offs, out):
         nc.vector.memset(head_ones[HEAD:P, HEAD:P], 1.0)
 
         a = [[held.tile([P, PIECE], BF16, name=f"a{k}_{j}") for j in range(PIECES)] for k in range(BLOCKS)]
-        for k in range(BLOCKS):
-            for j in range(PIECES):
-                picked = work.tile([P, PIECE], F32, name="picked")
-                nc.scalar.activation(
-                    picked[:],
-                    table[k][:].indirect(offsets[:, j * OFFS_COLS : (j + 1) * OFFS_COLS]),
-                    ACT.Copy,
-                )
-                nc.vector.scalar_tensor_tensor(
-                    out=a[k][j][:], in0=picked[:], scalar=SLOPE, in1=picked[:], op0=ALU.mult, op1=ALU.max
-                )
 
-        for j in range(PIECES):
-            cols = slice(j * PIECE, (j + 1) * PIECE)
-            for part, name in enumerate(("q", "k", "v")):
-                for m in range(BLOCKS):
-                    rows = slice(part * D + m * P, part * D + (m + 1) * P)
-                    product = products.tile([P, PIECE], F32, name="product")
-                    for k in range(BLOCKS):
-                        nc.tensor.matmul(
-                            product[:],
-                            weights[name][:, k, m * P : (m + 1) * P],
-                            a[k][j][:],
-                            start=(k == 0),
-                            stop=(k == BLOCKS - 1),
-                        )
-                    low = work.tile([P, PIECE], F32, name="low")
-                    nc.scalar.activation(
-                        low[:], product[:], ACT.Identity, bias=low_bias[name][:, m : m + 1], scale=SLOPE
-                    )
-                    hidden = work.tile([P, PIECE], F32, name="hidden")
-                    nc.vector.scalar_tensor_tensor(
-                        out=hidden[:],
-                        in0=product[:],
-                        scalar=bias[name][:, m : m + 1],
-                        in1=low[:],
-                        op0=ALU.add,
-                        op1=ALU.max,
-                    )
-                    if name == "v":
-                        nc.sync.dma_start(out[rows, cols], hidden[:])
-                        continue
-                    squares = work.tile([P, PIECE], BF16, name="squares")
-                    nc.gpsimd.tensor_tensor(squares[:], hidden[:], hidden[:], ALU.mult)
-                    length2 = lengths.tile([P, PIECE], F32, name="length2")
-                    nc.tensor.matmul(length2[:], head_ones[:], squares[:], start=True, stop=True)
-                    inverse = work.tile([P, PIECE], F32, name="inverse")
-                    nc.scalar.activation(inverse[:], length2[:], ACT.Abs_reciprocal_sqrt)
-                    unit = work.tile([P, PIECE], F32, name="unit")
-                    nc.vector.tensor_tensor(unit[:], hidden[:], inverse[:], ALU.mult)
-                    nc.sync.dma_start(out[rows, cols], unit[:])
+        def look_up(k, j):
+            picked = work.tile([P, PIECE], F32, name="picked")
+            nc.scalar.activation(
+                picked[:],
+                table[k][:].indirect(offsets[:, j * OFFS_COLS : (j + 1) * OFFS_COLS]),
+                ACT.Copy,
+            )
+            nc.vector.scalar_tensor_tensor(
+                out=a[k][j][:], in0=picked[:], scalar=SLOPE, in1=picked[:], op0=ALU.mult, op1=ALU.max
+            )
+
+        def project(j, part, m):
+            name = ("q", "k", "v")[part]
+            where = out[part * D + m * P : part * D + (m + 1) * P, j * PIECE : (j + 1) * PIECE]
+            product = products.tile([P, PIECE], F32, name="product")
+            for k in range(BLOCKS):
+                nc.tensor.matmul(
+                    product[:],
+                    weights[name][:, k, m * P : (m + 1) * P],
+                    a[k][j][:],
+                    start=(k == 0),
+                    stop=(k == BLOCKS - 1),
+                )
+            low = work.tile([P, PIECE], F32, name="low")
+            nc.scalar.activation(low[:], product[:], ACT.Identity, bias=low_bias[name][:, m : m + 1], scale=SLOPE)
+            hidden = kept.tile([P, PIECE], F32, name="hidden")
+            nc.vector.scalar_tensor_tensor(
+                out=hidden[:], in0=product[:], scalar=bias[name][:, m : m + 1], in1=low[:], op0=ALU.add, op1=ALU.max
+            )
+            if name == "v":
+                nc.sync.dma_start(where, hidden[:])
+                return None
+            squares = kept.tile([P, PIECE], BF16, name="squares")
+            nc.gpsimd.tensor_tensor(squares[:], hidden[:], hidden[:], ALU.mult)
+            return where, hidden, squares
+
+        def normalise(where, hidden, squares):
+            length2 = lengths.tile([P, PIECE], F32, name="length2")
+            nc.tensor.matmul(length2[:], head_ones[:], squares[:], start=True, stop=True)
+            inverse = work.tile([P, PIECE], F32, name="inverse")
+            nc.scalar.activation(inverse[:], length2[:], ACT.Abs_reciprocal_sqrt)
+            unit = work.tile([P, PIECE], F32, name="unit")
+            nc.vector.tensor_tensor(unit[:], hidden[:], inverse[:], ALU.mult)
+            nc.sync.dma_start(where, unit[:])
+
+        units = [(j, part, m) for j in range(PIECES) for part in range(3) for m in range(BLOCKS)]
+        units_per_look_up = 3 * BLOCKS // BLOCKS
+        for k in range(BLOCKS):
+            look_up(k, 0)
+        projected = []
+        for i, (j, part, m) in enumerate(units):
+            in_piece = part * BLOCKS + m
+            if j + 1 < PIECES and in_piece % units_per_look_up == 0:
+                look_up(in_piece // units_per_look_up, j + 1)
+            projected.append(project(j, part, m))
+            if i >= LAG and projected[i - LAG] is not None:
+                normalise(*projected[i - LAG])
+        for late in projected[len(units) - LAG :]:
+            if late is not None:
+                normalise(*late)

@@ -16,7 +16,9 @@ BLOCKS = D // P
 PIECE = 512
 PIECES = N // PIECE
 OFFS_COLS = PIECE // 16
-LAG = 3
+GROUP = 2 * P
+GROUPS = D // GROUP
+LAG = 2
 
 FLOPS = 2 * 3 * D * D * N
 
@@ -26,41 +28,38 @@ def tile_etcmodel_b_kernel(tc, emb, w_q, b_q, w_k, b_k, w_v, b_v, offs, out):
     with (
         tc.tile_pool(name="held", bufs=1) as held,
         tc.tile_pool(name="work", bufs=4) as work,
-        tc.tile_pool(name="kept", bufs=LAG + 3) as kept,
-        tc.psum_pool(name="products", bufs=6) as products,
-        tc.psum_pool(name="lengths", bufs=2) as lengths,
+        tc.tile_pool(name="kept", bufs=2 * (LAG + 2)) as kept,
+        tc.psum_pool(name="products", bufs=7) as products,
+        tc.psum_pool(name="lengths", bufs=1) as lengths,
     ):
         offsets = held.tile([P, N // 16], U16, name="offsets")
         nc.sync.dma_start(offsets[:], offs)
 
+        emb_blocks = emb.rearrange("(p k) s -> p k s", k=BLOCKS)
         table = [held.tile([P, S], F32, name=f"table{k}") for k in range(BLOCKS)]
         weights = {}
         for name in ("q", "k", "v"):
             weights[name] = held.tile([P, BLOCKS, D], BF16, name=f"w_{name}")
 
-        def load_weights(name, w):
-            nc.sync.dma_start(weights[name][:], w.rearrange("(k p) m -> p k m", p=P))
-
-        nc.sync.dma_start(table[0][:], emb[0:P, :])
-        load_weights("q", w_q)
-        for k in range(1, BLOCKS):
-            nc.sync.dma_start(table[k][:], emb[k * P : (k + 1) * P, :])
-        load_weights("k", w_k)
-        load_weights("v", w_v)
+        nc.gpsimd.dma_start(weights["q"][:], w_q.rearrange("(p k) m -> p k m", k=BLOCKS))
+        for k in range(BLOCKS):
+            nc.sync.dma_start(table[k][:], emb_blocks[:, k, :])
+        nc.sync.dma_start(weights["k"][:], w_k.rearrange("(p k) m -> p k m", k=BLOCKS))
+        nc.sync.dma_start(weights["v"][:], w_v.rearrange("(p k) m -> p k m", k=BLOCKS))
 
         bias = {}
         low_bias = {}
         for name, b in (("q", b_q), ("k", b_k), ("v", b_v)):
-            bias[name] = held.tile([P, BLOCKS], F32, name=f"b_{name}")
-            with nc.allow_non_contiguous_dma(reason="one bias value to a partition"):
-                nc.scalar.dma_start(bias[name][:], b.rearrange("(a p) o -> p (a o)", p=P))
-            low_bias[name] = held.tile([P, BLOCKS], F32, name=f"low_b_{name}")
+            bias[name] = held.tile([P, GROUPS, 2], F32, name=f"b_{name}")
+            with nc.allow_non_contiguous_dma(reason="two neighbouring bias values to a partition and group"):
+                nc.scalar.dma_start(bias[name][:], b.rearrange("(g p s) o -> p g (s o)", p=P, s=2))
+            low_bias[name] = held.tile([P, GROUPS, 2], F32, name=f"low_b_{name}")
             nc.vector.tensor_scalar_mul(low_bias[name][:], bias[name][:], SLOPE)
 
         head_ones = held.tile([P, P], BF16, name="head_ones")
         nc.vector.memset(head_ones[:], 0.0)
-        nc.vector.memset(head_ones[0:HEAD, 0:HEAD], 1.0)
-        nc.vector.memset(head_ones[HEAD:P, HEAD:P], 1.0)
+        for first in range(0, P, HEAD // 2):
+            nc.vector.memset(head_ones[first : first + HEAD // 2, first : first + HEAD // 2], 1.0)
 
         a = [[held.tile([P, PIECE], BF16, name=f"a{k}_{j}") for j in range(PIECES)] for k in range(BLOCKS)]
 
@@ -75,52 +74,66 @@ def tile_etcmodel_b_kernel(tc, emb, w_q, b_q, w_k, b_k, w_v, b_v, offs, out):
                 out=a[k][j][:], in0=picked[:], scalar=SLOPE, in1=picked[:], op0=ALU.mult, op1=ALU.max
             )
 
-        def project(j, part, m):
+        def project(j, part, g):
             name = ("q", "k", "v")[part]
-            where = out[part * D + m * P : part * D + (m + 1) * P, j * PIECE : (j + 1) * PIECE]
-            product = products.tile([P, PIECE], F32, name="product")
-            for k in range(BLOCKS):
-                nc.tensor.matmul(
-                    product[:],
-                    weights[name][:, k, m * P : (m + 1) * P],
-                    a[k][j][:],
-                    start=(k == 0),
-                    stop=(k == BLOCKS - 1),
+            sisters = []
+            for s in range(2):
+                features = slice(GROUP * g + s, GROUP * (g + 1), 2)
+                where = out[part * D + features.start : part * D + features.stop : 2, j * PIECE : (j + 1) * PIECE]
+                product = products.tile([P, PIECE], F32, name="product")
+                for k in range(BLOCKS):
+                    nc.tensor.matmul(
+                        product[:],
+                        weights[name][:, k, features],
+                        a[k][j][:],
+                        start=(k == 0),
+                        stop=(k == BLOCKS - 1),
+                    )
+                low = work.tile([P, PIECE], F32, name="low")
+                nc.scalar.activation(
+                    low[:], product[:], ACT.Identity, bias=low_bias[name][:, g, s : s + 1], scale=SLOPE
                 )
-            low = work.tile([P, PIECE], F32, name="low")
-            nc.scalar.activation(low[:], product[:], ACT.Identity, bias=low_bias[name][:, m : m + 1], scale=SLOPE)
-            hidden = kept.tile([P, PIECE], F32, name="hidden")
-            nc.vector.scalar_tensor_tensor(
-                out=hidden[:], in0=product[:], scalar=bias[name][:, m : m + 1], in1=low[:], op0=ALU.add, op1=ALU.max
-            )
+                hidden = kept.tile([P, PIECE], F32, name="hidden")
+                nc.vector.scalar_tensor_tensor(
+                    out=hidden[:], in0=product[:], scalar=bias[name][:, g, s : s + 1], in1=low[:],
+                    op0=ALU.add, op1=ALU.max,
+                )
+                if name == "v":
+                    nc.sync.dma_start(where, hidden[:])
+                sisters.append((where, hidden))
             if name == "v":
-                nc.sync.dma_start(where, hidden[:])
                 return None
+            even2 = work.tile([P, PIECE], F32, name="even2")
+            nc.gpsimd.tensor_tensor(even2[:], sisters[0][1][:], sisters[0][1][:], ALU.mult)
+            odd2 = work.tile([P, PIECE], F32, name="odd2")
+            nc.scalar.activation(odd2[:], sisters[1][1][:], ACT.Square)
             squares = kept.tile([P, PIECE], BF16, name="squares")
-            nc.gpsimd.tensor_tensor(squares[:], hidden[:], hidden[:], ALU.mult)
-            return where, hidden, squares
+            nc.vector.tensor_tensor(squares[:], even2[:], odd2[:], ALU.add)
+            return sisters, squares
 
-        def normalise(where, hidden, squares):
+        def normalise(sisters, squares):
             length2 = lengths.tile([P, PIECE], F32, name="length2")
             nc.tensor.matmul(length2[:], head_ones[:], squares[:], start=True, stop=True)
             inverse = work.tile([P, PIECE], F32, name="inverse")
             nc.scalar.activation(inverse[:], length2[:], ACT.Abs_reciprocal_sqrt)
-            unit = work.tile([P, PIECE], F32, name="unit")
-            nc.vector.tensor_tensor(unit[:], hidden[:], inverse[:], ALU.mult)
-            nc.sync.dma_start(where, unit[:])
+            for where, hidden in sisters:
+                unit = work.tile([P, PIECE], F32, name="unit")
+                nc.vector.tensor_tensor(unit[:], hidden[:], inverse[:], ALU.mult)
+                nc.sync.dma_start(where, unit[:])
 
-        units = [(j, part, m) for j in range(PIECES) for part in range(3) for m in range(BLOCKS)]
-        units_per_look_up = 3 * BLOCKS // BLOCKS
-        for k in range(BLOCKS):
-            look_up(k, 0)
+        for k in range(BLOCKS - 1):
+            for j in range(PIECES):
+                look_up(k, j)
+        look_up(BLOCKS - 1, 0)
+
+        pairs = [(j, part, g) for j in range(PIECES) for part in range(3) for g in range(GROUPS)]
         projected = []
-        for i, (j, part, m) in enumerate(units):
-            in_piece = part * BLOCKS + m
-            if j + 1 < PIECES and in_piece % units_per_look_up == 0:
-                look_up(in_piece // units_per_look_up, j + 1)
-            projected.append(project(j, part, m))
-            if i >= LAG and projected[i - LAG] is not None:
-                normalise(*projected[i - LAG])
-        for late in projected[len(units) - LAG :]:
+        for t, (j, part, g) in enumerate(pairs):
+            projected.append(project(j, part, g))
+            if t + 1 < PIECES:
+                look_up(BLOCKS - 1, t + 1)
+            if t >= LAG and projected[t - LAG] is not None:
+                normalise(*projected[t - LAG])
+        for late in projected[len(pairs) - LAG :]:
             if late is not None:
                 normalise(*late)

@@ -19,6 +19,9 @@ OFFS_COLS = PIECE // 16
 GROUP = 2 * P
 GROUPS = D // GROUP
 LAG = 2
+AHEAD = {1: 4}
+FIRST_BORROWER = ("q", 0, 0, 1)
+HIDDEN_TILES = 14
 
 FLOPS = 2 * 3 * D * D * N
 
@@ -27,6 +30,7 @@ def tile_etcmodel_b_kernel(tc, emb, w_q, b_q, w_k, b_k, w_v, b_v, offs, out):
     nc = tc.nc
     with (
         tc.tile_pool(name="held", bufs=1) as held,
+        tc.tile_pool(name="blocks", bufs=BLOCKS) as blocks,
         tc.tile_pool(name="work", bufs=4) as work,
         tc.tile_pool(name="kept", bufs=2 * (LAG + 2)) as kept,
         tc.psum_pool(name="products", bufs=7) as products,
@@ -36,14 +40,15 @@ def tile_etcmodel_b_kernel(tc, emb, w_q, b_q, w_k, b_k, w_v, b_v, offs, out):
         nc.sync.dma_start(offsets[:], offs)
 
         emb_blocks = emb.rearrange("(p k) s -> p k s", k=BLOCKS)
-        table = [held.tile([P, S], F32, name=f"table{k}") for k in range(BLOCKS)]
+        table = [blocks.tile([P, S], F32, name=f"table{k}", tag="block") for k in range(BLOCKS)]
         weights = {}
         for name in ("q", "k", "v"):
             weights[name] = held.tile([P, BLOCKS, D], BF16, name=f"w_{name}")
 
-        nc.gpsimd.dma_start(weights["q"][:], w_q.rearrange("(p k) m -> p k m", k=BLOCKS))
         for k in range(BLOCKS):
             nc.sync.dma_start(table[k][:], emb_blocks[:, k, :])
+            if k == 0:
+                nc.sync.dma_start(weights["q"][:], w_q.rearrange("(p k) m -> p k m", k=BLOCKS))
         nc.sync.dma_start(weights["k"][:], w_k.rearrange("(p k) m -> p k m", k=BLOCKS))
         nc.sync.dma_start(weights["v"][:], w_v.rearrange("(p k) m -> p k m", k=BLOCKS))
 
@@ -74,30 +79,55 @@ def tile_etcmodel_b_kernel(tc, emb, w_q, b_q, w_k, b_k, w_v, b_v, offs, out):
                 out=a[k][j][:], in0=picked[:], scalar=SLOPE, in1=picked[:], op0=ALU.mult, op1=ALU.max
             )
 
+        def multiply(name, j, g, s, some_blocks):
+            if (name, j, g, s) == FIRST_BORROWER:
+                product = lengths.tile([P, PIECE], F32, name="length2")
+            else:
+                product = products.tile([P, PIECE], F32, name="product")
+            for k in some_blocks:
+                nc.tensor.matmul(
+                    product[:],
+                    weights[name][:, k, GROUP * g + s : GROUP * (g + 1) : 2],
+                    a[k][j][:],
+                    start=(k == some_blocks[0]),
+                    stop=(k == some_blocks[-1]),
+                )
+            return product
+
+        parked = {}
+
+        def begin_ahead(j):
+            store = blocks.tile([P, S], F32, name="store", tag="block")
+            for g in range(GROUPS):
+                for s in range(2):
+                    product = multiply("q", j, g, s, range(AHEAD[j]))
+                    parked[j, g, s] = store[:, (2 * g + s) * PIECE : (2 * g + s + 1) * PIECE]
+                    nc.vector.tensor_scalar_add(parked[j, g, s], product[:], bias["q"][:, g, s : s + 1])
+
         def project(j, part, g):
             name = ("q", "k", "v")[part]
             sisters = []
             for s in range(2):
                 features = slice(GROUP * g + s, GROUP * (g + 1), 2)
                 where = out[part * D + features.start : part * D + features.stop : 2, j * PIECE : (j + 1) * PIECE]
-                product = products.tile([P, PIECE], F32, name="product")
-                for k in range(BLOCKS):
-                    nc.tensor.matmul(
-                        product[:],
-                        weights[name][:, k, features],
-                        a[k][j][:],
-                        start=(k == 0),
-                        stop=(k == BLOCKS - 1),
+                hidden = kept.tile([P, PIECE], F32, name="hidden", bufs=HIDDEN_TILES)
+                if name == "q" and j in AHEAD:
+                    product = multiply(name, j, g, s, range(AHEAD[j], BLOCKS))
+                    whole = work.tile([P, PIECE], F32, name="whole", bufs=2)
+                    nc.vector.tensor_tensor(whole[:], product[:], parked[j, g, s], ALU.add)
+                    nc.vector.scalar_tensor_tensor(
+                        out=hidden[:], in0=whole[:], scalar=SLOPE, in1=whole[:], op0=ALU.mult, op1=ALU.max
                     )
-                low = work.tile([P, PIECE], F32, name="low")
-                nc.scalar.activation(
-                    low[:], product[:], ACT.Identity, bias=low_bias[name][:, g, s : s + 1], scale=SLOPE
-                )
-                hidden = kept.tile([P, PIECE], F32, name="hidden")
-                nc.vector.scalar_tensor_tensor(
-                    out=hidden[:], in0=product[:], scalar=bias[name][:, g, s : s + 1], in1=low[:],
-                    op0=ALU.add, op1=ALU.max,
-                )
+                else:
+                    product = multiply(name, j, g, s, range(BLOCKS))
+                    low = work.tile([P, PIECE], F32, name="low")
+                    nc.scalar.activation(
+                        low[:], product[:], ACT.Identity, bias=low_bias[name][:, g, s : s + 1], scale=SLOPE
+                    )
+                    nc.vector.scalar_tensor_tensor(
+                        out=hidden[:], in0=product[:], scalar=bias[name][:, g, s : s + 1], in1=low[:],
+                        op0=ALU.add, op1=ALU.max,
+                    )
                 if name == "v":
                     nc.sync.dma_start(where, hidden[:])
                 sisters.append((where, hidden))
@@ -125,6 +155,9 @@ def tile_etcmodel_b_kernel(tc, emb, w_q, b_q, w_k, b_k, w_v, b_v, offs, out):
             for j in range(PIECES):
                 look_up(k, j)
         look_up(BLOCKS - 1, 0)
+
+        for j in AHEAD:
+            begin_ahead(j)
 
         pairs = [(j, part, g) for j in range(PIECES) for part in range(3) for g in range(GROUPS)]
         projected = []

@@ -19,9 +19,8 @@ OFFS_COLS = PIECE // 16
 GROUP = 2 * P
 GROUPS = D // GROUP
 LAG = 2
-AHEAD = {1: 4}
-FIRST_BORROWER = ("q", 0, 0, 1)
-HIDDEN_TILES = 14
+AHEAD = ((1, 0), (2, 0), (3, 0))
+EARLY = 4
 
 FLOPS = 2 * 3 * D * D * N
 
@@ -31,6 +30,7 @@ def tile_etcmodel_b_kernel(tc, emb, w_q, b_q, w_k, b_k, w_v, b_v, offs, out):
     with (
         tc.tile_pool(name="held", bufs=1) as held,
         tc.tile_pool(name="blocks", bufs=BLOCKS) as blocks,
+        tc.tile_pool(name="turns", bufs=2) as turns,
         tc.tile_pool(name="work", bufs=4) as work,
         tc.tile_pool(name="kept", bufs=2 * (LAG + 2)) as kept,
         tc.psum_pool(name="products", bufs=7) as products,
@@ -66,9 +66,13 @@ def tile_etcmodel_b_kernel(tc, emb, w_q, b_q, w_k, b_k, w_v, b_v, offs, out):
         for first in range(0, P, HEAD // 2):
             nc.vector.memset(head_ones[first : first + HEAD // 2, first : first + HEAD // 2], 1.0)
 
-        a = [[held.tile([P, PIECE], BF16, name=f"a{k}_{j}") for j in range(PIECES)] for k in range(BLOCKS)]
+        a = [{} for k in range(BLOCKS)]
 
         def look_up(k, j):
+            if k < EARLY:
+                a[k][j] = held.tile([P, PIECE], BF16, name=f"a{k}_{j}")
+            else:
+                a[k][j] = turns.tile([P, PIECE], BF16, name=f"a{k}_{j}", tag=f"a{k}")
             picked = work.tile([P, PIECE], F32, name="picked")
             nc.scalar.activation(
                 picked[:],
@@ -80,10 +84,7 @@ def tile_etcmodel_b_kernel(tc, emb, w_q, b_q, w_k, b_k, w_v, b_v, offs, out):
             )
 
         def multiply(name, j, g, s, some_blocks):
-            if (name, j, g, s) == FIRST_BORROWER:
-                product = lengths.tile([P, PIECE], F32, name="length2")
-            else:
-                product = products.tile([P, PIECE], F32, name="product")
+            product = products.tile([P, PIECE], F32, name="product")
             for k in some_blocks:
                 nc.tensor.matmul(
                     product[:],
@@ -96,12 +97,12 @@ def tile_etcmodel_b_kernel(tc, emb, w_q, b_q, w_k, b_k, w_v, b_v, offs, out):
 
         parked = {}
 
-        def begin_ahead(j):
+        def begin_ahead():
             store = blocks.tile([P, S], F32, name="store", tag="block")
-            for g in range(GROUPS):
+            for t, (j, g) in enumerate(AHEAD):
                 for s in range(2):
-                    product = multiply("q", j, g, s, range(AHEAD[j]))
-                    parked[j, g, s] = store[:, (2 * g + s) * PIECE : (2 * g + s + 1) * PIECE]
+                    product = multiply("q", j, g, s, range(EARLY))
+                    parked[j, g, s] = store[:, (2 * t + s) * PIECE : (2 * t + s + 1) * PIECE]
                     nc.vector.tensor_scalar_add(parked[j, g, s], product[:], bias["q"][:, g, s : s + 1])
 
         def project(j, part, g):
@@ -110,9 +111,9 @@ def tile_etcmodel_b_kernel(tc, emb, w_q, b_q, w_k, b_k, w_v, b_v, offs, out):
             for s in range(2):
                 features = slice(GROUP * g + s, GROUP * (g + 1), 2)
                 where = out[part * D + features.start : part * D + features.stop : 2, j * PIECE : (j + 1) * PIECE]
-                hidden = kept.tile([P, PIECE], F32, name="hidden", bufs=HIDDEN_TILES)
-                if name == "q" and j in AHEAD:
-                    product = multiply(name, j, g, s, range(AHEAD[j], BLOCKS))
+                hidden = kept.tile([P, PIECE], F32, name="hidden")
+                if name == "q" and (j, g) in AHEAD:
+                    product = multiply(name, j, g, s, range(EARLY, BLOCKS))
                     whole = work.tile([P, PIECE], F32, name="whole", bufs=2)
                     nc.vector.tensor_tensor(whole[:], product[:], parked[j, g, s], ALU.add)
                     nc.vector.scalar_tensor_tensor(
@@ -151,20 +152,21 @@ def tile_etcmodel_b_kernel(tc, emb, w_q, b_q, w_k, b_k, w_v, b_v, offs, out):
                 nc.vector.tensor_tensor(unit[:], hidden[:], inverse[:], ALU.mult)
                 nc.sync.dma_start(where, unit[:])
 
-        for k in range(BLOCKS - 1):
+        for k in range(EARLY):
             for j in range(PIECES):
                 look_up(k, j)
-        look_up(BLOCKS - 1, 0)
+        for k in range(EARLY, BLOCKS):
+            look_up(k, 0)
+        late_look_ups = [(k, j) for j in range(1, PIECES) for k in range(EARLY, BLOCKS)]
 
-        for j in AHEAD:
-            begin_ahead(j)
+        begin_ahead()
 
         pairs = [(j, part, g) for j in range(PIECES) for part in range(3) for g in range(GROUPS)]
         projected = []
         for t, (j, part, g) in enumerate(pairs):
             projected.append(project(j, part, g))
-            if t + 1 < PIECES:
-                look_up(BLOCKS - 1, t + 1)
+            if t < len(late_look_ups):
+                look_up(*late_look_ups[t])
             if t >= LAG and projected[t - LAG] is not None:
                 normalise(*projected[t - LAG])
         for late in projected[len(pairs) - LAG :]:

@@ -21,6 +21,7 @@ GROUPS = D // GROUP
 LAG = 2
 AHEAD = ((1, 0), (2, 0), (3, 0))
 EARLY = 4
+FIRST_BORROWER = ("q", 0, 0, 1)
 
 FLOPS = 2 * 3 * D * D * N
 
@@ -66,6 +67,11 @@ def tile_etcmodel_b_kernel(tc, emb, w_q, b_q, w_k, b_k, w_v, b_v, offs, out):
         for first in range(0, P, HEAD // 2):
             nc.vector.memset(head_ones[first : first + HEAD // 2, first : first + HEAD // 2], 1.0)
 
+        ones = held.tile([P, 1], F32, name="ones")
+        nc.vector.memset(ones[:], 1.0)
+        warmed = held.tile([P, 1], F32, name="warmed")
+        nc.scalar.activation(warmed[:], ones[:], ACT.Abs_reciprocal_sqrt)
+
         a = [{} for k in range(BLOCKS)]
 
         def look_up(k, j):
@@ -84,7 +90,10 @@ def tile_etcmodel_b_kernel(tc, emb, w_q, b_q, w_k, b_k, w_v, b_v, offs, out):
             )
 
         def multiply(name, j, g, s, some_blocks):
-            product = products.tile([P, PIECE], F32, name="product")
+            if (name, j, g, s) == FIRST_BORROWER:
+                product = lengths.tile([P, PIECE], F32, name="length2")
+            else:
+                product = products.tile([P, PIECE], F32, name="product")
             for k in some_blocks:
                 nc.tensor.matmul(
                     product[:],

@@ -1,4 +1,5 @@
 import concourse.mybir as mybir
+from concourse.masks import make_block_diagonal
 
 F32 = mybir.dt.float32
 BF16 = mybir.dt.bfloat16
@@ -16,12 +17,12 @@ BLOCKS = D // P
 PIECE = 512
 PIECES = N // PIECE
 OFFS_COLS = PIECE // 16
-GROUP = 2 * P
-GROUPS = D // GROUP
-LAG = 2
-AHEAD = ((1, 0), (2, 0), (3, 0))
+GROUPS = ((0, 4), (4 * P, 2))
+LAG = 3
+AHEAD = ((1, 1), (2, 1), (3, 1))
 EARLY = 4
 FIRST_BORROWER = ("q", 0, 0, 1)
+HIDDEN_TILES = 16
 
 FLOPS = 2 * 3 * D * D * N
 
@@ -33,7 +34,7 @@ def tile_etcmodel_b_kernel(tc, emb, w_q, b_q, w_k, b_k, w_v, b_v, offs, out):
         tc.tile_pool(name="blocks", bufs=BLOCKS) as blocks,
         tc.tile_pool(name="turns", bufs=2) as turns,
         tc.tile_pool(name="work", bufs=4) as work,
-        tc.tile_pool(name="kept", bufs=2 * (LAG + 2)) as kept,
+        tc.tile_pool(name="kept", bufs=LAG + 2) as kept,
         tc.psum_pool(name="products", bufs=7) as products,
         tc.psum_pool(name="lengths", bufs=1) as lengths,
     ):
@@ -53,19 +54,28 @@ def tile_etcmodel_b_kernel(tc, emb, w_q, b_q, w_k, b_k, w_v, b_v, offs, out):
         nc.sync.dma_start(weights["k"][:], w_k.rearrange("(p k) m -> p k m", k=BLOCKS))
         nc.sync.dma_start(weights["v"][:], w_v.rearrange("(p k) m -> p k m", k=BLOCKS))
 
+        def features_of(g, s):
+            first, sisters = GROUPS[g]
+            return slice(first + s, first + sisters * P, sisters)
+
         bias = {}
         low_bias = {}
         for name, b in (("q", b_q), ("k", b_k), ("v", b_v)):
-            bias[name] = held.tile([P, GROUPS, 2], F32, name=f"b_{name}")
-            with nc.allow_non_contiguous_dma(reason="two neighbouring bias values to a partition and group"):
-                nc.scalar.dma_start(bias[name][:], b.rearrange("(g p s) o -> p g (s o)", p=P, s=2))
-            low_bias[name] = held.tile([P, GROUPS, 2], F32, name=f"low_b_{name}")
-            nc.vector.tensor_scalar_mul(low_bias[name][:], bias[name][:], SLOPE)
+            for g, (first, sisters) in enumerate(GROUPS):
+                bias[name, g] = held.tile([P, sisters], F32, name=f"b_{name}{g}")
+                with nc.allow_non_contiguous_dma(reason="a few neighbouring bias values to a partition"):
+                    nc.scalar.dma_start(
+                        bias[name, g][:], b[first : first + sisters * P, :].rearrange("(p s) o -> p (s o)", s=sisters)
+                    )
+                low_bias[name, g] = held.tile([P, sisters], F32, name=f"low_b_{name}{g}")
+                nc.vector.tensor_scalar_mul(low_bias[name, g][:], bias[name, g][:], SLOPE)
 
-        head_ones = held.tile([P, P], BF16, name="head_ones")
-        nc.vector.memset(head_ones[:], 0.0)
-        for first in range(0, P, HEAD // 2):
-            nc.vector.memset(head_ones[first : first + HEAD // 2, first : first + HEAD // 2], 1.0)
+        head_ones = []
+        for g, (first, sisters) in enumerate(GROUPS):
+            blocks_of_ones = held.tile([P, P], F32, name=f"blocks_of_ones{g}")
+            make_block_diagonal(nc, blocks_of_ones[:], HEAD // sisters)
+            head_ones.append(held.tile([P, P], BF16, name=f"head_ones{g}"))
+            nc.vector.tensor_copy(head_ones[g][:], blocks_of_ones[:])
 
         ones = held.tile([P, 1], F32, name="ones")
         nc.vector.memset(ones[:], 1.0)
@@ -97,7 +107,7 @@ def tile_etcmodel_b_kernel(tc, emb, w_q, b_q, w_k, b_k, w_v, b_v, offs, out):
             for k in some_blocks:
                 nc.tensor.matmul(
                     product[:],
-                    weights[name][:, k, GROUP * g + s : GROUP * (g + 1) : 2],
+                    weights[name][:, k, features_of(g, s)],
                     a[k][j][:],
                     start=(k == some_blocks[0]),
                     stop=(k == some_blocks[-1]),
@@ -112,15 +122,17 @@ def tile_etcmodel_b_kernel(tc, emb, w_q, b_q, w_k, b_k, w_v, b_v, offs, out):
                 for s in range(2):
                     product = multiply("q", j, g, s, range(EARLY))
                     parked[j, g, s] = store[:, (2 * t + s) * PIECE : (2 * t + s + 1) * PIECE]
-                    nc.vector.tensor_scalar_add(parked[j, g, s], product[:], bias["q"][:, g, s : s + 1])
+                    nc.vector.tensor_scalar_add(parked[j, g, s], product[:], bias["q", g][:, s : s + 1])
 
         def project(j, part, g):
             name = ("q", "k", "v")[part]
             sisters = []
-            for s in range(2):
-                features = slice(GROUP * g + s, GROUP * (g + 1), 2)
-                where = out[part * D + features.start : part * D + features.stop : 2, j * PIECE : (j + 1) * PIECE]
-                hidden = kept.tile([P, PIECE], F32, name="hidden")
+            for s in range(GROUPS[g][1]):
+                features = features_of(g, s)
+                where = out[
+                    part * D + features.start : part * D + features.stop : features.step, j * PIECE : (j + 1) * PIECE
+                ]
+                hidden = kept.tile([P, PIECE], F32, name="hidden", bufs=HIDDEN_TILES)
                 if name == "q" and (j, g) in AHEAD:
                     product = multiply(name, j, g, s, range(EARLY, BLOCKS))
                     whole = work.tile([P, PIECE], F32, name="whole", bufs=2)
@@ -132,10 +144,10 @@ def tile_etcmodel_b_kernel(tc, emb, w_q, b_q, w_k, b_k, w_v, b_v, offs, out):
                     product = multiply(name, j, g, s, range(BLOCKS))
                     low = work.tile([P, PIECE], F32, name="low")
                     nc.scalar.activation(
-                        low[:], product[:], ACT.Identity, bias=low_bias[name][:, g, s : s + 1], scale=SLOPE
+                        low[:], product[:], ACT.Identity, bias=low_bias[name, g][:, s : s + 1], scale=SLOPE
                     )
                     nc.vector.scalar_tensor_tensor(
-                        out=hidden[:], in0=product[:], scalar=bias[name][:, g, s : s + 1], in1=low[:],
+                        out=hidden[:], in0=product[:], scalar=bias[name, g][:, s : s + 1], in1=low[:],
                         op0=ALU.add, op1=ALU.max,
                     )
                 if name == "v":
@@ -143,17 +155,24 @@ def tile_etcmodel_b_kernel(tc, emb, w_q, b_q, w_k, b_k, w_v, b_v, offs, out):
                 sisters.append((where, hidden))
             if name == "v":
                 return None
-            even2 = work.tile([P, PIECE], F32, name="even2")
-            nc.gpsimd.tensor_tensor(even2[:], sisters[0][1][:], sisters[0][1][:], ALU.mult)
-            odd2 = work.tile([P, PIECE], F32, name="odd2")
-            nc.scalar.activation(odd2[:], sisters[1][1][:], ACT.Square)
-            squares = kept.tile([P, PIECE], BF16, name="squares")
-            nc.vector.tensor_tensor(squares[:], even2[:], odd2[:], ALU.add)
-            return sisters, squares
+            squares = None
+            for s, (where, hidden) in enumerate(sisters):
+                square = work.tile([P, PIECE], F32, name="square")
+                nc.scalar.activation(square[:], hidden[:], ACT.Square)
+                if s == 0:
+                    squares = square
+                    continue
+                if s == len(sisters) - 1:
+                    longer = kept.tile([P, PIECE], BF16, name="squares")
+                else:
+                    longer = work.tile([P, PIECE], F32, name="partial", bufs=3)
+                nc.vector.tensor_tensor(longer[:], squares[:], square[:], ALU.add)
+                squares = longer
+            return g, sisters, squares
 
-        def normalise(sisters, squares):
+        def normalise(g, sisters, squares):
             length2 = lengths.tile([P, PIECE], F32, name="length2")
-            nc.tensor.matmul(length2[:], head_ones[:], squares[:], start=True, stop=True)
+            nc.tensor.matmul(length2[:], head_ones[g][:], squares[:], start=True, stop=True)
             inverse = work.tile([P, PIECE], F32, name="inverse")
             nc.scalar.activation(inverse[:], length2[:], ACT.Abs_reciprocal_sqrt)
             for where, hidden in sisters:
@@ -170,7 +189,7 @@ def tile_etcmodel_b_kernel(tc, emb, w_q, b_q, w_k, b_k, w_v, b_v, offs, out):
 
         begin_ahead()
 
-        pairs = [(j, part, g) for j in range(PIECES) for part in range(3) for g in range(GROUPS)]
+        pairs = [(j, part, g) for j in range(PIECES) for part in range(3) for g in range(len(GROUPS))]
         projected = []
         for t, (j, part, g) in enumerate(pairs):
             projected.append(project(j, part, g))

@@ -18,11 +18,12 @@ PIECE = 512
 PIECES = N // PIECE
 OFFS_COLS = PIECE // 16
 GROUPS = ((0, 4), (4 * P, 2))
-LAG = 3
+LAG = 24
 AHEAD = ((1, 1), (2, 1), (3, 1))
 EARLY = 4
 FIRST_BORROWER = ("q", 0, 0, 1)
 HIDDEN_TILES = 16
+SQUARES_TILES = 4
 
 FLOPS = 2 * 3 * D * D * N
 
@@ -34,7 +35,7 @@ def tile_etcmodel_b_kernel(tc, emb, w_q, b_q, w_k, b_k, w_v, b_v, offs, out):
         tc.tile_pool(name="blocks", bufs=BLOCKS) as blocks,
         tc.tile_pool(name="turns", bufs=2) as turns,
         tc.tile_pool(name="work", bufs=4) as work,
-        tc.tile_pool(name="kept", bufs=LAG + 2) as kept,
+        tc.tile_pool(name="kept", bufs=SQUARES_TILES) as kept,
         tc.psum_pool(name="products", bufs=7) as products,
         tc.psum_pool(name="lengths", bufs=1) as lengths,
     ):
@@ -99,11 +100,15 @@ def tile_etcmodel_b_kernel(tc, emb, w_q, b_q, w_k, b_k, w_v, b_v, offs, out):
                 out=a[k][j][:], in0=picked[:], scalar=SLOPE, in1=picked[:], op0=ALU.mult, op1=ALU.max
             )
 
+        written = {"matmuls": 0, "normalised": 0}
+        waiting = []
+
         def multiply(name, j, g, s, some_blocks):
             if (name, j, g, s) == FIRST_BORROWER:
                 product = lengths.tile([P, PIECE], F32, name="length2")
             else:
                 product = products.tile([P, PIECE], F32, name="product")
+            written["matmuls"] += len(some_blocks)
             for k in some_blocks:
                 nc.tensor.matmul(
                     product[:],
@@ -153,8 +158,9 @@ def tile_etcmodel_b_kernel(tc, emb, w_q, b_q, w_k, b_k, w_v, b_v, offs, out):
                 if name == "v":
                     nc.sync.dma_start(where, hidden[:])
                 sisters.append((where, hidden))
+                catch_up(LAG)
             if name == "v":
-                return None
+                return
             squares = None
             for s, (where, hidden) in enumerate(sisters):
                 square = work.tile([P, PIECE], F32, name="square")
@@ -168,7 +174,7 @@ def tile_etcmodel_b_kernel(tc, emb, w_q, b_q, w_k, b_k, w_v, b_v, offs, out):
                     longer = work.tile([P, PIECE], F32, name="partial", bufs=3)
                 nc.vector.tensor_tensor(longer[:], squares[:], square[:], ALU.add)
                 squares = longer
-            return g, sisters, squares
+            waiting.append((written["matmuls"], g, sisters, squares))
 
         def normalise(g, sisters, squares):
             length2 = lengths.tile([P, PIECE], F32, name="length2")
@@ -180,6 +186,14 @@ def tile_etcmodel_b_kernel(tc, emb, w_q, b_q, w_k, b_k, w_v, b_v, offs, out):
                 nc.vector.tensor_tensor(unit[:], hidden[:], inverse[:], ALU.mult)
                 nc.sync.dma_start(where, unit[:])
 
+        def catch_up(lag):
+            while written["normalised"] < len(waiting):
+                since, g, sisters, squares = waiting[written["normalised"]]
+                if written["matmuls"] - since < lag:
+                    break
+                normalise(g, sisters, squares)
+                written["normalised"] += 1
+
         for k in range(EARLY):
             for j in range(PIECES):
                 look_up(k, j)
@@ -190,13 +204,8 @@ def tile_etcmodel_b_kernel(tc, emb, w_q, b_q, w_k, b_k, w_v, b_v, offs, out):
         begin_ahead()
 
         pairs = [(j, part, g) for j in range(PIECES) for part in range(3) for g in range(len(GROUPS))]
-        projected = []
         for t, (j, part, g) in enumerate(pairs):
-            projected.append(project(j, part, g))
+            project(j, part, g)
             if t < len(late_look_ups):
                 look_up(*late_look_ups[t])
-            if t >= LAG and projected[t - LAG] is not None:
-                normalise(*projected[t - LAG])
-        for late in projected[len(pairs) - LAG :]:
-            if late is not None:
-                normalise(*late)
+        catch_up(0)

@@ -19,8 +19,9 @@ PIECES = N // PIECE
 OFFS_COLS = PIECE // 16
 GROUPS = ((0, 4), (4 * P, 2))
 LAG = 24
-AHEAD = ((1, 1), (2, 1), (3, 1))
+AHEAD = ((1, 1), (2, 1))
 EARLY = 4
+SOON = 3
 FIRST_BORROWER = ("q", 0, 0, 1)
 HIDDEN_TILES = 16
 SQUARES_TILES = 4
@@ -86,10 +87,7 @@ def tile_etcmodel_b_kernel(tc, emb, w_q, b_q, w_k, b_k, w_v, b_v, offs, out):
         a = [{} for k in range(BLOCKS)]
 
         def look_up(k, j):
-            if k < EARLY:
-                a[k][j] = held.tile([P, PIECE], BF16, name=f"a{k}_{j}")
-            else:
-                a[k][j] = turns.tile([P, PIECE], BF16, name=f"a{k}_{j}", tag=f"a{k}")
+            a[k][j] = turns.tile([P, PIECE], BF16, name=f"a{k}_{j}", tag=f"a{k}", bufs=SOON if k < EARLY else 2)
             picked = work.tile([P, PIECE], F32, name="picked")
             nc.scalar.activation(
                 picked[:],
@@ -122,7 +120,7 @@ def tile_etcmodel_b_kernel(tc, emb, w_q, b_q, w_k, b_k, w_v, b_v, offs, out):
         parked = {}
 
         def begin_ahead():
-            store = blocks.tile([P, S], F32, name="store", tag="block")
+            store = held.tile([P, 2 * len(AHEAD) * PIECE], F32, name="store")
             for t, (j, g) in enumerate(AHEAD):
                 for s in range(2):
                     product = multiply("q", j, g, s, range(EARLY))
@@ -195,17 +193,21 @@ def tile_etcmodel_b_kernel(tc, emb, w_q, b_q, w_k, b_k, w_v, b_v, offs, out):
                 written["normalised"] += 1
 
         for k in range(EARLY):
-            for j in range(PIECES):
+            for j in range(SOON):
                 look_up(k, j)
         for k in range(EARLY, BLOCKS):
             look_up(k, 0)
-        late_look_ups = [(k, j) for j in range(1, PIECES) for k in range(EARLY, BLOCKS)]
+            look_up(k, 1)
+        put_off = [(k, 2) for k in range(EARLY, BLOCKS)] + [(k, j) for j in range(SOON, PIECES) for k in range(BLOCKS)]
 
         begin_ahead()
 
         pairs = [(j, part, g) for j in range(PIECES) for part in range(3) for g in range(len(GROUPS))]
+        pairs.remove((1, 0, 0))
+        pairs.insert(2, (1, 0, 0))
+        FIRST_PUT_OFF = pairs.index((0, 2, 1)) + 1
         for t, (j, part, g) in enumerate(pairs):
             project(j, part, g)
-            if t < len(late_look_ups):
-                look_up(*late_look_ups[t])
+            if FIRST_PUT_OFF <= t < FIRST_PUT_OFF + len(put_off):
+                look_up(*put_off[t - FIRST_PUT_OFF])
         catch_up(0)

@@ -18,7 +18,8 @@ PIECE = 512
 PIECES = N // PIECE
 OFFS_COLS = PIECE // 16
 GROUPS = ((0, 4), (4 * P, 2))
-LAG = 24
+LAG = 48
+LAST_LAG = 24
 AHEAD = ((1, 1), (2, 1))
 EARLY = 4
 SOON = 3
@@ -156,7 +157,7 @@ def tile_etcmodel_b_kernel(tc, emb, w_q, b_q, w_k, b_k, w_v, b_v, offs, out):
                 if name == "v":
                     nc.sync.dma_start(where, hidden[:])
                 sisters.append((where, hidden))
-                catch_up(LAG)
+                catch_up()
             if name == "v":
                 return
             squares = None
@@ -172,7 +173,7 @@ def tile_etcmodel_b_kernel(tc, emb, w_q, b_q, w_k, b_k, w_v, b_v, offs, out):
                     longer = work.tile([P, PIECE], F32, name="partial", bufs=3)
                 nc.vector.tensor_tensor(longer[:], squares[:], square[:], ALU.add)
                 squares = longer
-            waiting.append((written["matmuls"], g, sisters, squares))
+            waiting.append((written["matmuls"] + (LAG if j < PIECES - 1 else LAST_LAG), g, sisters, squares))
 
         def normalise(g, sisters, squares):
             length2 = lengths.tile([P, PIECE], F32, name="length2")
@@ -184,10 +185,10 @@ def tile_etcmodel_b_kernel(tc, emb, w_q, b_q, w_k, b_k, w_v, b_v, offs, out):
                 nc.vector.tensor_tensor(unit[:], hidden[:], inverse[:], ALU.mult)
                 nc.sync.dma_start(where, unit[:])
 
-        def catch_up(lag):
+        def catch_up():
             while written["normalised"] < len(waiting):
-                since, g, sisters, squares = waiting[written["normalised"]]
-                if written["matmuls"] - since < lag:
+                due, g, sisters, squares = waiting[written["normalised"]]
+                if written["matmuls"] < due:
                     break
                 normalise(g, sisters, squares)
                 written["normalised"] += 1
@@ -210,4 +211,4 @@ def tile_etcmodel_b_kernel(tc, emb, w_q, b_q, w_k, b_k, w_v, b_v, offs, out):
             project(j, part, g)
             if FIRST_PUT_OFF <= t < FIRST_PUT_OFF + len(put_off):
                 look_up(*put_off[t - FIRST_PUT_OFF])
-        catch_up(0)
+        assert written["normalised"] == len(waiting)

@@ -17,13 +17,13 @@ BLOCKS = D // P
 PIECE = 512
 PIECES = N // PIECE
 OFFS_COLS = PIECE // 16
-GROUPS = ((0, 4), (4 * P, 2))
+GROUPS = {"few": (0, 4), "many": (4 * P, 8), "values": (2 * D, 6)}
 LAG = 48
 LAST_LAG = 24
-AHEAD = ((1, 1), (2, 1))
+AHEAD = (2, "few")
 EARLY = 4
 SOON = 3
-FIRST_BORROWER = ("q", 0, 0, 1)
+FIRST_BORROWER = (0, "few", 1)
 HIDDEN_TILES = 16
 SQUARES_TILES = 4
 
@@ -46,39 +46,45 @@ def tile_etcmodel_b_kernel(tc, emb, w_q, b_q, w_k, b_k, w_v, b_v, offs, out):
 
         emb_blocks = emb.rearrange("(p k) s -> p k s", k=BLOCKS)
         table = [blocks.tile([P, S], F32, name=f"table{k}", tag="block") for k in range(BLOCKS)]
+        q_blocks = w_q.rearrange("(p k) m -> p k m", k=BLOCKS)
+        k_blocks = w_k.rearrange("(p k) m -> p k m", k=BLOCKS)
+        v_blocks = w_v.rearrange("(p k) m -> p k m", k=BLOCKS)
         weights = {}
-        for name in ("q", "k", "v"):
-            weights[name] = held.tile([P, BLOCKS, D], BF16, name=f"w_{name}")
+        for name in GROUPS:
+            weights[name] = held.tile([P, BLOCKS, GROUPS[name][1] * P], BF16, name=f"w_{name}")
+        few_rows = GROUPS["many"][0]
+        other_rows = D - few_rows
 
         for k in range(BLOCKS):
             nc.sync.dma_start(table[k][:], emb_blocks[:, k, :])
             if k == 0:
-                nc.sync.dma_start(weights["q"][:], w_q.rearrange("(p k) m -> p k m", k=BLOCKS))
-        nc.sync.dma_start(weights["k"][:], w_k.rearrange("(p k) m -> p k m", k=BLOCKS))
-        nc.sync.dma_start(weights["v"][:], w_v.rearrange("(p k) m -> p k m", k=BLOCKS))
-
-        def features_of(g, s):
-            first, sisters = GROUPS[g]
-            return slice(first + s, first + sisters * P, sisters)
+                nc.sync.dma_start(weights["few"][:], q_blocks[:, :, 0:few_rows])
+        nc.sync.dma_start(weights["many"][:, :, 0:other_rows], q_blocks[:, :, few_rows:D])
+        nc.sync.dma_start(weights["many"][:, :, other_rows : other_rows + D], k_blocks)
+        nc.sync.dma_start(weights["values"][:], v_blocks)
 
         bias = {}
+        for name in GROUPS:
+            bias[name] = held.tile([P, GROUPS[name][1]], F32, name=f"b_{name}")
+        many = GROUPS["many"][1]
+        with nc.allow_non_contiguous_dma(reason="a few neighbouring bias values to a partition"):
+            nc.scalar.dma_start(bias["few"][:], b_q[0:few_rows, :].rearrange("(p s) o -> p (s o)", s=GROUPS["few"][1]))
+            nc.scalar.dma_start(
+                bias["many"][0 : other_rows // many, :], b_q[few_rows:D, :].rearrange("(p s) o -> p (s o)", s=many)
+            )
+            nc.scalar.dma_start(bias["many"][other_rows // many : P, :], b_k.rearrange("(p s) o -> p (s o)", s=many))
+            nc.scalar.dma_start(bias["values"][:], b_v.rearrange("(p s) o -> p (s o)", s=GROUPS["values"][1]))
         low_bias = {}
-        for name, b in (("q", b_q), ("k", b_k), ("v", b_v)):
-            for g, (first, sisters) in enumerate(GROUPS):
-                bias[name, g] = held.tile([P, sisters], F32, name=f"b_{name}{g}")
-                with nc.allow_non_contiguous_dma(reason="a few neighbouring bias values to a partition"):
-                    nc.scalar.dma_start(
-                        bias[name, g][:], b[first : first + sisters * P, :].rearrange("(p s) o -> p (s o)", s=sisters)
-                    )
-                low_bias[name, g] = held.tile([P, sisters], F32, name=f"low_b_{name}{g}")
-                nc.vector.tensor_scalar_mul(low_bias[name, g][:], bias[name, g][:], SLOPE)
+        for name in GROUPS:
+            low_bias[name] = held.tile([P, GROUPS[name][1]], F32, name=f"low_b_{name}")
+            nc.vector.tensor_scalar_mul(low_bias[name][:], bias[name][:], SLOPE)
 
-        head_ones = []
-        for g, (first, sisters) in enumerate(GROUPS):
-            blocks_of_ones = held.tile([P, P], F32, name=f"blocks_of_ones{g}")
-            make_block_diagonal(nc, blocks_of_ones[:], HEAD // sisters)
-            head_ones.append(held.tile([P, P], BF16, name=f"head_ones{g}"))
-            nc.vector.tensor_copy(head_ones[g][:], blocks_of_ones[:])
+        head_ones = {}
+        for name in ("few", "many"):
+            blocks_of_ones = held.tile([P, P], F32, name=f"blocks_of_ones_{name}")
+            make_block_diagonal(nc, blocks_of_ones[:], HEAD // GROUPS[name][1])
+            head_ones[name] = held.tile([P, P], BF16, name=f"head_ones_{name}")
+            nc.vector.tensor_copy(head_ones[name][:], blocks_of_ones[:])
 
         ones = held.tile([P, 1], F32, name="ones")
         nc.vector.memset(ones[:], 1.0)
@@ -102,63 +108,63 @@ def tile_etcmodel_b_kernel(tc, emb, w_q, b_q, w_k, b_k, w_v, b_v, offs, out):
         written = {"matmuls": 0, "normalised": 0}
         waiting = []
 
-        def multiply(name, j, g, s, some_blocks):
-            if (name, j, g, s) == FIRST_BORROWER:
+        def multiply(j, name, s, some_blocks):
+            if (j, name, s) == FIRST_BORROWER:
                 product = lengths.tile([P, PIECE], F32, name="length2")
             else:
                 product = products.tile([P, PIECE], F32, name="product")
+            sisters = GROUPS[name][1]
             written["matmuls"] += len(some_blocks)
             for k in some_blocks:
                 nc.tensor.matmul(
                     product[:],
-                    weights[name][:, k, features_of(g, s)],
+                    weights[name][:, k, s : sisters * P : sisters],
                     a[k][j][:],
                     start=(k == some_blocks[0]),
                     stop=(k == some_blocks[-1]),
                 )
             return product
 
-        parked = {}
+        parked = []
 
         def begin_ahead():
-            store = held.tile([P, 2 * len(AHEAD) * PIECE], F32, name="store")
-            for t, (j, g) in enumerate(AHEAD):
-                for s in range(2):
-                    product = multiply("q", j, g, s, range(EARLY))
-                    parked[j, g, s] = store[:, (2 * t + s) * PIECE : (2 * t + s + 1) * PIECE]
-                    nc.vector.tensor_scalar_add(parked[j, g, s], product[:], bias["q", g][:, s : s + 1])
+            j, name = AHEAD
+            store = held.tile([P, GROUPS[name][1] * PIECE], F32, name="store")
+            for s in range(GROUPS[name][1]):
+                product = multiply(j, name, s, range(EARLY))
+                parked.append(store[:, s * PIECE : (s + 1) * PIECE])
+                nc.vector.tensor_scalar_add(parked[s], product[:], bias[name][:, s : s + 1])
 
-        def project(j, part, g):
-            name = ("q", "k", "v")[part]
+        def project(j, name, behind_units=()):
+            first, n = GROUPS[name]
             sisters = []
-            for s in range(GROUPS[g][1]):
-                features = features_of(g, s)
-                where = out[
-                    part * D + features.start : part * D + features.stop : features.step, j * PIECE : (j + 1) * PIECE
-                ]
+            for s in range(n):
+                where = out[first + s : first + n * P : n, j * PIECE : (j + 1) * PIECE]
                 hidden = kept.tile([P, PIECE], F32, name="hidden", bufs=HIDDEN_TILES)
-                if name == "q" and (j, g) in AHEAD:
-                    product = multiply(name, j, g, s, range(EARLY, BLOCKS))
+                if (j, name) == AHEAD:
+                    product = multiply(j, name, s, range(EARLY, BLOCKS))
                     whole = work.tile([P, PIECE], F32, name="whole", bufs=2)
-                    nc.vector.tensor_tensor(whole[:], product[:], parked[j, g, s], ALU.add)
+                    nc.vector.tensor_tensor(whole[:], product[:], parked[s], ALU.add)
                     nc.vector.scalar_tensor_tensor(
                         out=hidden[:], in0=whole[:], scalar=SLOPE, in1=whole[:], op0=ALU.mult, op1=ALU.max
                     )
                 else:
-                    product = multiply(name, j, g, s, range(BLOCKS))
+                    product = multiply(j, name, s, range(BLOCKS))
                     low = work.tile([P, PIECE], F32, name="low")
                     nc.scalar.activation(
-                        low[:], product[:], ACT.Identity, bias=low_bias[name, g][:, s : s + 1], scale=SLOPE
+                        low[:], product[:], ACT.Identity, bias=low_bias[name][:, s : s + 1], scale=SLOPE
                     )
                     nc.vector.scalar_tensor_tensor(
-                        out=hidden[:], in0=product[:], scalar=bias[name, g][:, s : s + 1], in1=low[:],
+                        out=hidden[:], in0=product[:], scalar=bias[name][:, s : s + 1], in1=low[:],
                         op0=ALU.add, op1=ALU.max,
                     )
-                if name == "v":
+                if name == "values":
                     nc.sync.dma_start(where, hidden[:])
                 sisters.append((where, hidden))
+                if s < len(behind_units):
+                    look_up(*behind_units[s])
                 catch_up()
-            if name == "v":
+            if name == "values":
                 return
             squares = None
             for s, (where, hidden) in enumerate(sisters):
@@ -167,17 +173,17 @@ def tile_etcmodel_b_kernel(tc, emb, w_q, b_q, w_k, b_k, w_v, b_v, offs, out):
                 if s == 0:
                     squares = square
                     continue
-                if s == len(sisters) - 1:
+                if s == n - 1:
                     longer = kept.tile([P, PIECE], BF16, name="squares")
                 else:
                     longer = work.tile([P, PIECE], F32, name="partial", bufs=3)
                 nc.vector.tensor_tensor(longer[:], squares[:], square[:], ALU.add)
                 squares = longer
-            waiting.append((written["matmuls"] + (LAG if j < PIECES - 1 else LAST_LAG), g, sisters, squares))
+            waiting.append((written["matmuls"] + (LAG if j < PIECES - 1 else LAST_LAG), name, sisters, squares))
 
-        def normalise(g, sisters, squares):
+        def normalise(name, sisters, squares):
             length2 = lengths.tile([P, PIECE], F32, name="length2")
-            nc.tensor.matmul(length2[:], head_ones[g][:], squares[:], start=True, stop=True)
+            nc.tensor.matmul(length2[:], head_ones[name][:], squares[:], start=True, stop=True)
             inverse = work.tile([P, PIECE], F32, name="inverse")
             nc.scalar.activation(inverse[:], length2[:], ACT.Abs_reciprocal_sqrt)
             for where, hidden in sisters:
@@ -187,10 +193,10 @@ def tile_etcmodel_b_kernel(tc, emb, w_q, b_q, w_k, b_k, w_v, b_v, offs, out):
 
         def catch_up():
             while written["normalised"] < len(waiting):
-                due, g, sisters, squares = waiting[written["normalised"]]
+                due, name, sisters, squares = waiting[written["normalised"]]
                 if written["matmuls"] < due:
                     break
-                normalise(g, sisters, squares)
+                normalise(name, sisters, squares)
                 written["normalised"] += 1
 
         for k in range(EARLY):
@@ -203,12 +209,14 @@ def tile_etcmodel_b_kernel(tc, emb, w_q, b_q, w_k, b_k, w_v, b_v, offs, out):
 
         begin_ahead()
 
-        pairs = [(j, part, g) for j in range(PIECES) for part in range(3) for g in range(len(GROUPS))]
-        pairs.remove((1, 0, 0))
-        pairs.insert(2, (1, 0, 0))
-        FIRST_PUT_OFF = pairs.index((0, 2, 1)) + 1
-        for t, (j, part, g) in enumerate(pairs):
-            project(j, part, g)
-            if FIRST_PUT_OFF <= t < FIRST_PUT_OFF + len(put_off):
-                look_up(*put_off[t - FIRST_PUT_OFF])
+        project(0, "few")
+        project(1, "few")
+        project(0, "many")
+        project(0, "values")
+        project(1, "many", behind_units=put_off)
+        project(1, "values")
+        for j in range(2, PIECES):
+            project(j, "many")
+            project(j, "few")
+            project(j, "values")
         assert written["normalised"] == len(waiting)

@@ -24,7 +24,7 @@ AHEAD = (2, "few")
 EARLY = 4
 SOON = 3
 FIRST_BORROWER = (0, "few", 1)
-HIDDEN_TILES = 16
+HIDDEN_TILES = 20
 SQUARES_TILES = 4
 
 FLOPS = 2 * 3 * D * D * N
@@ -59,9 +59,9 @@ def tile_etcmodel_b_kernel(tc, emb, w_q, b_q, w_k, b_k, w_v, b_v, offs, out):
             nc.sync.dma_start(table[k][:], emb_blocks[:, k, :])
             if k == 0:
                 nc.sync.dma_start(weights["few"][:], q_blocks[:, :, 0:few_rows])
+        nc.sync.dma_start(weights["values"][:], v_blocks)
         nc.sync.dma_start(weights["many"][:, :, 0:other_rows], q_blocks[:, :, few_rows:D])
         nc.sync.dma_start(weights["many"][:, :, other_rows : other_rows + D], k_blocks)
-        nc.sync.dma_start(weights["values"][:], v_blocks)
 
         bias = {}
         for name in GROUPS:
@@ -77,7 +77,7 @@ def tile_etcmodel_b_kernel(tc, emb, w_q, b_q, w_k, b_k, w_v, b_v, offs, out):
         low_bias = {}
         for name in GROUPS:
             low_bias[name] = held.tile([P, GROUPS[name][1]], F32, name=f"low_b_{name}")
-            nc.vector.tensor_scalar_mul(low_bias[name][:], bias[name][:], SLOPE)
+            nc.gpsimd.tensor_scalar_mul(low_bias[name][:], bias[name][:], SLOPE)
 
         head_ones = {}
         for name in ("few", "many"):
@@ -187,9 +187,8 @@ def tile_etcmodel_b_kernel(tc, emb, w_q, b_q, w_k, b_k, w_v, b_v, offs, out):
             inverse = work.tile([P, PIECE], F32, name="inverse")
             nc.scalar.activation(inverse[:], length2[:], ACT.Abs_reciprocal_sqrt)
             for where, hidden in sisters:
-                unit = work.tile([P, PIECE], F32, name="unit")
-                nc.vector.tensor_tensor(unit[:], hidden[:], inverse[:], ALU.mult)
-                nc.sync.dma_start(where, unit[:])
+                nc.vector.tensor_tensor(hidden[:], hidden[:], inverse[:], ALU.mult)
+                nc.sync.dma_start(where, hidden[:])
 
         def catch_up():
             while written["normalised"] < len(waiting):
@@ -211,8 +210,8 @@ def tile_etcmodel_b_kernel(tc, emb, w_q, b_q, w_k, b_k, w_v, b_v, offs, out):
 
         project(0, "few")
         project(1, "few")
-        project(0, "many")
         project(0, "values")
+        project(0, "many")
         project(1, "many", behind_units=put_off)
         project(1, "values")
         for j in range(2, PIECES):

@@ -24,7 +24,7 @@ AHEAD = (2, "few")
 EARLY = 4
 SOON = 3
 FIRST_BORROWER = (0, "few", 1)
-HIDDEN_TILES = 20
+HIDDEN_TILES = 24
 SQUARES_TILES = 4
 
 FLOPS = 2 * 3 * D * D * N
@@ -59,25 +59,20 @@ def tile_etcmodel_b_kernel(tc, emb, w_q, b_q, w_k, b_k, w_v, b_v, offs, out):
             nc.sync.dma_start(table[k][:], emb_blocks[:, k, :])
             if k == 0:
                 nc.sync.dma_start(weights["few"][:], q_blocks[:, :, 0:few_rows])
-        nc.sync.dma_start(weights["values"][:], v_blocks)
-        nc.sync.dma_start(weights["many"][:, :, 0:other_rows], q_blocks[:, :, few_rows:D])
-        nc.sync.dma_start(weights["many"][:, :, other_rows : other_rows + D], k_blocks)
-
         bias = {}
         for name in GROUPS:
             bias[name] = held.tile([P, GROUPS[name][1]], F32, name=f"b_{name}")
         many = GROUPS["many"][1]
         with nc.allow_non_contiguous_dma(reason="a few neighbouring bias values to a partition"):
-            nc.scalar.dma_start(bias["few"][:], b_q[0:few_rows, :].rearrange("(p s) o -> p (s o)", s=GROUPS["few"][1]))
-            nc.scalar.dma_start(
+            nc.sync.dma_start(bias["few"][:], b_q[0:few_rows, :].rearrange("(p s) o -> p (s o)", s=GROUPS["few"][1]))
+            nc.sync.dma_start(bias["values"][:], b_v.rearrange("(p s) o -> p (s o)", s=GROUPS["values"][1]))
+            nc.sync.dma_start(
                 bias["many"][0 : other_rows // many, :], b_q[few_rows:D, :].rearrange("(p s) o -> p (s o)", s=many)
             )
-            nc.scalar.dma_start(bias["many"][other_rows // many : P, :], b_k.rearrange("(p s) o -> p (s o)", s=many))
-            nc.scalar.dma_start(bias["values"][:], b_v.rearrange("(p s) o -> p (s o)", s=GROUPS["values"][1]))
-        low_bias = {}
-        for name in GROUPS:
-            low_bias[name] = held.tile([P, GROUPS[name][1]], F32, name=f"low_b_{name}")
-            nc.gpsimd.tensor_scalar_mul(low_bias[name][:], bias[name][:], SLOPE)
+            nc.sync.dma_start(bias["many"][other_rows // many : P, :], b_k.rearrange("(p s) o -> p (s o)", s=many))
+        nc.sync.dma_start(weights["values"][:], v_blocks)
+        nc.sync.dma_start(weights["many"][:, :, 0:other_rows], q_blocks[:, :, few_rows:D])
+        nc.sync.dma_start(weights["many"][:, :, other_rows : other_rows + D], k_blocks)
 
         head_ones = {}
         for name in ("few", "many"):
@@ -133,7 +128,7 @@ def tile_etcmodel_b_kernel(tc, emb, w_q, b_q, w_k, b_k, w_v, b_v, offs, out):
             for s in range(GROUPS[name][1]):
                 product = multiply(j, name, s, range(EARLY))
                 parked.append(store[:, s * PIECE : (s + 1) * PIECE])
-                nc.vector.tensor_scalar_add(parked[s], product[:], bias[name][:, s : s + 1])
+                nc.vector.tensor_copy(parked[s], product[:])
 
         def project(j, name, behind_units=()):
             first, n = GROUPS[name]
@@ -143,21 +138,14 @@ def tile_etcmodel_b_kernel(tc, emb, w_q, b_q, w_k, b_k, w_v, b_v, offs, out):
                 hidden = kept.tile([P, PIECE], F32, name="hidden", bufs=HIDDEN_TILES)
                 if (j, name) == AHEAD:
                     product = multiply(j, name, s, range(EARLY, BLOCKS))
-                    whole = work.tile([P, PIECE], F32, name="whole", bufs=2)
-                    nc.vector.tensor_tensor(whole[:], product[:], parked[s], ALU.add)
-                    nc.vector.scalar_tensor_tensor(
-                        out=hidden[:], in0=whole[:], scalar=SLOPE, in1=whole[:], op0=ALU.mult, op1=ALU.max
-                    )
                 else:
                     product = multiply(j, name, s, range(BLOCKS))
-                    low = work.tile([P, PIECE], F32, name="low")
-                    nc.scalar.activation(
-                        low[:], product[:], ACT.Identity, bias=low_bias[name][:, s : s + 1], scale=SLOPE
-                    )
-                    nc.vector.scalar_tensor_tensor(
-                        out=hidden[:], in0=product[:], scalar=bias[name][:, s : s + 1], in1=low[:],
-                        op0=ALU.add, op1=ALU.max,
-                    )
+                nc.scalar.activation(hidden[:], product[:], ACT.Identity, bias=bias[name][:, s : s + 1])
+                if (j, name) == AHEAD:
+                    nc.vector.tensor_tensor(hidden[:], hidden[:], parked[s], ALU.add)
+                nc.vector.scalar_tensor_tensor(
+                    out=hidden[:], in0=hidden[:], scalar=SLOPE, in1=hidden[:], op0=ALU.mult, op1=ALU.max
+                )
                 if name == "values":
                     nc.sync.dma_start(where, hidden[:])
                 sisters.append((where, hidden))

import concourse.mybir as mybir
from concourse.masks import make_block_diagonal

F32 = mybir.dt.float32
BF16 = mybir.dt.bfloat16
U16 = mybir.dt.uint16
ACT = mybir.ActivationFunctionType
ALU = mybir.AluOpType

P = 128
D = 768
S = 4096
N = 2048
HEAD = 64
SLOPE = 0.01
BLOCKS = D // P
PIECE = 512
PIECES = N // PIECE
OFFS_COLS = PIECE // 16
GROUPS = {"few": (0, 4), "many": (4 * P, 8), "values": (2 * D, 6)}
LAG = 48
LAST_LAG = 24
AHEAD = (2, "few")
EARLY = 4
SOON = 3
FIRST_BORROWER = (0, "few", 1)
HIDDEN_TILES = 24
SQUARES_TILES = 4

FLOPS = 2 * 3 * D * D * N


def tile_etcmodel_b_kernel(tc, emb, w_q, b_q, w_k, b_k, w_v, b_v, offs, out):
    nc = tc.nc
    with (
        tc.tile_pool(name="held", bufs=1) as held,
        tc.tile_pool(name="blocks", bufs=BLOCKS) as blocks,
        tc.tile_pool(name="turns", bufs=2) as turns,
        tc.tile_pool(name="work", bufs=4) as work,
        tc.tile_pool(name="kept", bufs=SQUARES_TILES) as kept,
        tc.psum_pool(name="products", bufs=7) as products,
        tc.psum_pool(name="lengths", bufs=1) as lengths,
    ):
        offsets = held.tile([P, N // 16], U16, name="offsets")
        nc.sync.dma_start(offsets[:], offs)

        emb_blocks = emb.rearrange("(p k) s -> p k s", k=BLOCKS)
        table = [blocks.tile([P, S], F32, name=f"table{k}", tag="block") for k in range(BLOCKS)]
        q_blocks = w_q.rearrange("(p k) m -> p k m", k=BLOCKS)
        k_blocks = w_k.rearrange("(p k) m -> p k m", k=BLOCKS)
        v_blocks = w_v.rearrange("(p k) m -> p k m", k=BLOCKS)
        weights = {}
        for name in GROUPS:
            weights[name] = held.tile([P, BLOCKS, GROUPS[name][1] * P], BF16, name=f"w_{name}")
        few_rows = GROUPS["many"][0]
        other_rows = D - few_rows

        for k in range(BLOCKS):
            nc.sync.dma_start(table[k][:], emb_blocks[:, k, :])
            if k == 0:
                nc.sync.dma_start(weights["few"][:], q_blocks[:, :, 0:few_rows])
        bias = {}
        for name in GROUPS:
            bias[name] = held.tile([P, GROUPS[name][1]], F32, name=f"b_{name}")
        many = GROUPS["many"][1]
        with nc.allow_non_contiguous_dma(reason="a few neighbouring bias values to a partition"):
            nc.sync.dma_start(bias["few"][:], b_q[0:few_rows, :].rearrange("(p s) o -> p (s o)", s=GROUPS["few"][1]))
            nc.sync.dma_start(bias["values"][:], b_v.rearrange("(p s) o -> p (s o)", s=GROUPS["values"][1]))
            nc.sync.dma_start(
                bias["many"][0 : other_rows // many, :], b_q[few_rows:D, :].rearrange("(p s) o -> p (s o)", s=many)
            )
            nc.sync.dma_start(bias["many"][other_rows // many : P, :], b_k.rearrange("(p s) o -> p (s o)", s=many))
        nc.sync.dma_start(weights["values"][:], v_blocks)
        nc.sync.dma_start(weights["many"][:, :, 0:other_rows], q_blocks[:, :, few_rows:D])
        nc.sync.dma_start(weights["many"][:, :, other_rows : other_rows + D], k_blocks)

        head_ones = {}
        for name in ("few", "many"):
            blocks_of_ones = held.tile([P, P], F32, name=f"blocks_of_ones_{name}")
            make_block_diagonal(nc, blocks_of_ones[:], HEAD // GROUPS[name][1])
            head_ones[name] = held.tile([P, P], BF16, name=f"head_ones_{name}")
            nc.vector.tensor_copy(head_ones[name][:], blocks_of_ones[:])

        ones = held.tile([P, 1], F32, name="ones")
        nc.vector.memset(ones[:], 1.0)
        warmed = held.tile([P, 1], F32, name="warmed")
        nc.scalar.activation(warmed[:], ones[:], ACT.Abs_reciprocal_sqrt)

        a = [{} for k in range(BLOCKS)]

        def look_up(k, j):
            a[k][j] = turns.tile([P, PIECE], BF16, name=f"a{k}_{j}", tag=f"a{k}", bufs=SOON if k < EARLY else 2)
            picked = work.tile([P, PIECE], F32, name="picked")
            nc.scalar.activation(
                picked[:],
                table[k][:].indirect(offsets[:, j * OFFS_COLS : (j + 1) * OFFS_COLS]),
                ACT.Copy,
            )
            nc.vector.scalar_tensor_tensor(
                out=a[k][j][:], in0=picked[:], scalar=SLOPE, in1=picked[:], op0=ALU.mult, op1=ALU.max
            )

        written = {"matmuls": 0, "normalised": 0}
        waiting = []

        def multiply(j, name, s, some_blocks):
            if (j, name, s) == FIRST_BORROWER:
                product = lengths.tile([P, PIECE], F32, name="length2")
            else:
                product = products.tile([P, PIECE], F32, name="product")
            sisters = GROUPS[name][1]
            written["matmuls"] += len(some_blocks)
            for k in some_blocks:
                nc.tensor.matmul(
                    product[:],
                    weights[name][:, k, s : sisters * P : sisters],
                    a[k][j][:],
                    start=(k == some_blocks[0]),
                    stop=(k == some_blocks[-1]),
                )
            return product

        parked = []

        def begin_ahead():
            j, name = AHEAD
            store = held.tile([P, GROUPS[name][1] * PIECE], F32, name="store")
            for s in range(GROUPS[name][1]):
                product = multiply(j, name, s, range(EARLY))
                parked.append(store[:, s * PIECE : (s + 1) * PIECE])
                nc.vector.tensor_copy(parked[s], product[:])

        def project(j, name, behind_units=()):
            first, n = GROUPS[name]
            sisters = []
            for s in range(n):
                where = out[first + s : first + n * P : n, j * PIECE : (j + 1) * PIECE]
                hidden = kept.tile([P, PIECE], F32, name="hidden", bufs=HIDDEN_TILES)
                if (j, name) == AHEAD:
                    product = multiply(j, name, s, range(EARLY, BLOCKS))
                else:
                    product = multiply(j, name, s, range(BLOCKS))
                nc.scalar.activation(hidden[:], product[:], ACT.Identity, bias=bias[name][:, s : s + 1])
                if (j, name) == AHEAD:
                    nc.vector.tensor_tensor(hidden[:], hidden[:], parked[s], ALU.add)
                nc.vector.scalar_tensor_tensor(
                    out=hidden[:], in0=hidden[:], scalar=SLOPE, in1=hidden[:], op0=ALU.mult, op1=ALU.max
                )
                if name == "values":
                    nc.sync.dma_start(where, hidden[:])
                sisters.append((where, hidden))
                if s < len(behind_units):
                    look_up(*behind_units[s])
                catch_up()
            if name == "values":
                return
            squares = None
            for s, (where, hidden) in enumerate(sisters):
                square = work.tile([P, PIECE], F32, name="square")
                nc.scalar.activation(square[:], hidden[:], ACT.Square)
                if s == 0:
                    squares = square
                    continue
                if s == n - 1:
                    longer = kept.tile([P, PIECE], BF16, name="squares")
                else:
                    longer = work.tile([P, PIECE], F32, name="partial", bufs=3)
                nc.vector.tensor_tensor(longer[:], squares[:], square[:], ALU.add)
                squares = longer
            waiting.append((written["matmuls"] + (LAG if j < PIECES - 1 else LAST_LAG), name, sisters, squares))

        def normalise(name, sisters, squares):
            length2 = lengths.tile([P, PIECE], F32, name="length2")
            nc.tensor.matmul(length2[:], head_ones[name][:], squares[:], start=True, stop=True)
            inverse = work.tile([P, PIECE], F32, name="inverse")
            nc.scalar.activation(inverse[:], length2[:], ACT.Abs_reciprocal_sqrt)
            for where, hidden in sisters:
                nc.vector.tensor_tensor(hidden[:], hidden[:], inverse[:], ALU.mult)
                nc.sync.dma_start(where, hidden[:])

        def catch_up():
            while written["normalised"] < len(waiting):
                due, name, sisters, squares = waiting[written["normalised"]]
                if written["matmuls"] < due:
                    break
                normalise(name, sisters, squares)
                written["normalised"] += 1

        for k in range(EARLY):
            for j in range(SOON):
                look_up(k, j)
        for k in range(EARLY, BLOCKS):
            look_up(k, 0)
            look_up(k, 1)
        put_off = [(k, 2) for k in range(EARLY, BLOCKS)] + [(k, j) for j in range(SOON, PIECES) for k in range(BLOCKS)]

        begin_ahead()

        project(0, "few")
        project(1, "few")
        project(0, "values")
        project(0, "many")
        project(1, "many", behind_units=put_off)
        project(1, "values")
        for j in range(2, PIECES):
            project(j, "many")
            project(j, "few")
            project(j, "values")
        assert written["normalised"] == len(waiting)
